import numpy as np
import ml_dtypes


def mxq(x, axis, fmt="e4m3"):
    dtype, down = {"e4m3": (ml_dtypes.float8_e4m3fn, 7), "e5m2": (ml_dtypes.float8_e5m2, 14)}[fmt]
    v = np.moveaxis(np.asarray(x, np.float32).astype(ml_dtypes.bfloat16).astype(np.float64), axis, -1)
    blocks = v.reshape(v.shape[:-1] + (-1, 32))
    amax = np.abs(blocks).max(-1, keepdims=True)
    byte = np.maximum(np.where(amax > 0, np.frexp(amax)[1] - 1 + 127, 0) - down, 1)
    scale = np.exp2(byte - 127.0)
    codes = (blocks / scale).astype(np.float32).astype(dtype).astype(np.float64)
    return np.moveaxis((codes * scale).reshape(v.shape), -1, axis)


WIDE = False


def mx_kscale(k):
    if not WIDE:
        return np.ones(k)
    levels = np.array([10, -10, 5, -5, 0])
    if k % 512:
        return np.exp2(np.random.permutation(np.resize(levels, k // 32))).repeat(32)
    a = np.empty((k // 512, 16))
    for p in range(k // 512):
        a[p, :8] = np.random.permutation(np.resize(levels, 8))
        for g in range(8):
            far = levels[np.abs(levels - a[p, g]) >= 10]
            a[p, g + 8] = far[np.random.randint(len(far))]
    return np.exp2(a.ravel()).repeat(32)


BF16 = ml_dtypes.bfloat16


def bf(x):
    return np.asarray(x, np.float32).astype(BF16)


def f64(x):
    return np.asarray(x).astype(np.float64)


B, S, D, F, F2 = 4, 1024, 512, 512, 1024
EPS = 1e-6
D2 = 2 * D


def setup_inputs():
    n = np.random.standard_normal
    s, t = mx_kscale(F), mx_kscale(D2)
    tr, ti = t[:D], t[D:]
    wd = 1.5 / np.sqrt(F)
    return {'h_r': bf(n((B, S, F)) * 0.6 * s), 'h_i': bf(n((B, S, F)) * 0.6 * s),
            'w2r': bf(n((F, D)) * wd / s[:, None] * tr), 'b2r': bf(n(D) * 0.2 * tr),
            'w2i': bf(n((F, D)) * wd / s[:, None] * ti), 'b2i': bf(n(D) * 0.2 * ti),
            'We': bf(n((D2, D)) / np.sqrt(D2) / t[:, None]), 'be': bf(n(D) * 0.2),
            'g_rms': bf(1.0 + 0.1 * n(D))}


def reference(h_r, h_i, w2r, b2r, w2i, b2i, We, be, g_rms):
    rp = (mxq(f64(h_r), 2, 'e4m3') @ mxq(f64(w2r), 0, 'e4m3')) + f64(b2r)
    ip = (mxq(f64(h_i), 2, 'e4m3') @ mxq(f64(w2i), 0, 'e4m3')) + f64(b2i)
    cat = np.concatenate([rp, ip], axis=-1)
    wave = (mxq(cat, 2, 'e4m3') @ mxq(f64(We), 0, 'e4m3')) + f64(be)
    return wave * (1.0 / np.sqrt(np.mean(wave * wave, axis=-1, keepdims=True) + EPS)) * f64(g_rms)

@@ -1,0 +1,313 @@
+from contextlib import ExitStack
+
+import concourse.mybir as mybir
+from concourse.masks import make_identity
+
+F32 = mybir.dt.float32
+BF16 = mybir.dt.bfloat16
+U32 = mybir.dt.uint32
+U8 = mybir.dt.uint8
+FP8X4 = mybir.dt.float8_e4m3fn_x4
+ADD = mybir.AluOpType.add
+MULT = mybir.AluOpType.mult
+ACT = mybir.ActivationFunctionType
+
+P = 128
+PACK = 4
+TOKENS = 4096
+F = 512
+D = 512
+STREAMS = 2
+TILES = 2
+STEP_TOKENS = TILES * P
+STEPS = TOKENS // STEP_TOKENS
+PIECES = TILES * STREAMS
+EPS = 1e-6
+VECTOR_FINISHES = 2
+LOADS_BEFORE_BROADCASTS = 4
+
+FLOPS = 2 * TOKENS * F * D * STREAMS + 2 * TOKENS * (STREAMS * D) * D
+
+
+def tile_wavenetworklm_pb_t_kernel(tc, h_r, h_i, w2r, b2r, w2i, b2i, We, be, g_rms, out):
+    nc = tc.nc
+    h_dram = [h_r.flatten_outer_dims(), h_i.flatten_outer_dims()]
+    w2_dram = [w2r, w2i]
+    b2_dram = [b2r, b2i]
+    out_dram = out.flatten_outer_dims()
+
+    with ExitStack() as stack:
+        stack.enter_context(tc.manual_schedule())
+        keep = stack.enter_context(tc.tile_pool(name="keep", bufs=1))
+        work = stack.enter_context(tc.tile_pool(name="work", bufs=2))
+        tail = stack.enter_context(tc.tile_pool(name="tail", bufs=3))
+        psum_t = stack.enter_context(tc.psum_pool(name="psum_t", bufs=2))
+        psum_1 = stack.enter_context(tc.psum_pool(name="psum_1", bufs=4))
+        psum_2 = stack.enter_context(tc.psum_pool(name="psum_2", bufs=2))
+
+        def load_h(n):
+            rows = slice(n * STEP_TOKENS, (n + 1) * STEP_TOKENS)
+            tiles = []
+            for s in range(STREAMS):
+                h_sb = keep.tile([P, TILES * F], BF16, name="h_%d_%d" % (s, n))
+                nc.sync.dma_start(out=h_sb[:], in_=h_dram[s][rows, :].rearrange("(p k) f -> p (k f)", k=TILES))
+                tiles.append(h_sb)
+            return tiles
+
+        def load_w2(s):
+            raw = keep.tile([P, PACK, D], BF16, name="w2_raw_%d" % s)
+            nc.sync.dma_start(
+                out=raw[:].rearrange("q j d -> q (j d)"),
+                in_=w2_dram[s].rearrange("(q j) d -> q (j d)", j=PACK),
+            )
+            return raw
+
+        be_all = keep.tile([P, D], BF16)
+        gain_all = keep.tile([P, D], BF16)
+        w2_raw = [None, None]
+        h_tiles = {}
+        w2_raw[0] = load_w2(0)
+        h_tiles[0] = load_h(0)
+        w2_raw[1] = load_w2(1)
+        h_tiles[1] = load_h(1)
+        we_raw = keep.tile([P, STREAMS, PACK, D], BF16)
+        nc.sync.dma_start(
+            out=we_raw[:].rearrange("p s t d -> p s (t d)"),
+            in_=We.rearrange("(s p t) d -> p s (t d)", s=STREAMS, t=PACK),
+        )
+        for n in range(2, STEPS):
+            h_tiles[n] = load_h(n)
+            if n == LOADS_BEFORE_BROADCASTS:
+                nc.sync.dma_start(out=be_all[:], in_=be.partition_broadcast(P))
+                nc.sync.dma_start(out=gain_all[:], in_=g_rms.partition_broadcast(P))
+
+        identity = keep.tile([P, P], F32)
+        make_identity(nc, identity[:])
+        eps = keep.tile([P, 1], F32)
+        nc.vector.memset(eps[:], EPS)
+
+        b2 = []
+        for s in range(STREAMS):
+            b2_sb = keep.tile([P, PACK], BF16, name="b2_%d" % s)
+            nc.scalar.dma_start(out=b2_sb[:], in_=b2_dram[s].rearrange("(p t) -> p t", t=PACK))
+            b2.append(b2_sb)
+
+        w2_codes = []
+        w2_scales = []
+
+        def prepare_w2(s):
+            grouped = keep.tile([P, D * PACK], BF16, name="w2_grouped_%d" % s, align_bytes=64)
+            nc.vector.tensor_copy(
+                out=grouped[:].rearrange("q (t c j) -> q t c j", t=PACK, j=PACK),
+                in_=w2_raw[s][:].rearrange("q j (c t) -> q t c j", t=PACK),
+            )
+            return grouped
+
+        def quantise_w2(s, grouped):
+            codes = keep.tile([P, D], U32, name="w2_codes_%d" % s, align_bytes=64)
+            scales = keep.tile([P, D], U8, name="w2_scales_%d" % s, align_bytes=64)
+            nc.vector.quantize_mx(out=codes[:].bitcast(FP8X4), scales=scales[:], in_=grouped[:])
+            w2_codes.append(codes)
+            w2_scales.append(scales)
+
+        for s in range(STREAMS):
+            quantise_w2(s, prepare_w2(s))
+
+        we_grouped = keep.tile([P, STREAMS, D * PACK], BF16, align_bytes=64)
+        we_codes = keep.tile([P, STREAMS, D], U32, align_bytes=64)
+        we_scales = keep.tile([P, STREAMS, D], U8, align_bytes=64)
+
+        def regroup_we():
+            nc.scalar.copy(
+                out=we_grouped[:, 0, :].rearrange("p (d t) -> p d t", t=PACK),
+                in_=we_raw[:, 0, :, :].rearrange("p t d -> p d t"),
+            )
+            nc.gpsimd.tensor_scalar(
+                out=we_grouped[:, 1, :].rearrange("p (d t) -> p d t", t=PACK),
+                in0=we_raw[:, 1, :, :].rearrange("p t d -> p d t"),
+                scalar1=1.0,
+                scalar2=0.0,
+                op0=MULT,
+                op1=ADD,
+            )
+
+        def quantise_we():
+            nc.vector.quantize_mx(
+                out=we_codes[:].rearrange("p s d -> p (s d)").bitcast(FP8X4),
+                scales=we_scales[:].rearrange("p s d -> p (s d)"),
+                in_=we_grouped[:].rearrange("p s x -> p (s x)"),
+            )
+
+        h_words = {}
+        h_grouped = {}
+        h_codes = {}
+        sums_1 = {}
+        cat_grouped = {}
+        cat_codes = {}
+        sums_2 = {}
+        wave = {}
+        square_sums = {}
+        inv_rms = {}
+
+        def transposes(n):
+            for k in range(TILES):
+                words = psum_t.tile([P, STREAMS, 2, P], F32)
+                for s in range(STREAMS):
+                    source = h_tiles[n][s][:].bitcast(F32)
+                    for u in range(2):
+                        token = slice(k * (F // 2) + u, (k + 1) * (F // 2), 2)
+                        nc.tensor.transpose(words[:, s, u, :], source[:, token], identity[:])
+                h_words[(n, k)] = words
+
+        def copy_h(n):
+            grouped = work.tile([P, PIECES * P * PACK], BF16, align_bytes=64)
+            grouped_words = grouped[:].bitcast(F32)
+            width = STREAMS * P * 2
+            for k in range(TILES):
+                nc.scalar.copy(
+                    out=grouped_words[:, k * width : (k + 1) * width].rearrange("p (s r u) -> p s r u", s=STREAMS, u=2),
+                    in_=h_words[(n, k)][:].rearrange("p s u r -> p s r u"),
+                )
+            h_grouped[n] = grouped
+
+        def quantise(grouped, codes_name, scales_name):
+            codes = work.tile([P, PIECES * P], U32, name=codes_name, align_bytes=64)
+            scales = work.tile([P, PIECES * P], U8, name=scales_name, align_bytes=64)
+            nc.vector.quantize_mx(out=codes[:].bitcast(FP8X4), scales=scales[:], in_=grouped[:])
+            return codes, scales
+
+        def quantise_h(n):
+            h_codes[n] = quantise(h_grouped[n], "h_codes", "h_scales")
+
+        def stage_1(n, piece):
+            s = piece % STREAMS
+            codes, scales = h_codes[n]
+            tokens = slice(piece * P, (piece + 1) * P)
+            sums = psum_1.tile([P, PACK, P], F32)
+            for t in range(PACK):
+                columns = slice(t * P, (t + 1) * P)
+                nc.tensor.matmul_mx(
+                    out=sums[:, t, :],
+                    lhsT=w2_codes[s][:, columns].bitcast(FP8X4),
+                    lhsT_scale=w2_scales[s][:, columns],
+                    rhs=codes[:, tokens].bitcast(FP8X4),
+                    rhs_scale=scales[:, tokens],
+                    start=True,
+                    stop=True,
+                )
+            sums_1[(n, piece)] = sums
+
+        def new_cat(n):
+            cat = work.tile([P, PIECES * P * PACK], BF16, align_bytes=64)
+            cat_grouped[n] = cat
+
+        def bias_and_round(n, piece):
+            s = piece % STREAMS
+            width = P * PACK
+            nc.vector.tensor_tensor(
+                out=cat_grouped[n][:, piece * width : (piece + 1) * width].rearrange("p (r t) -> p r t", t=PACK),
+                in0=sums_1[(n, piece)][:].rearrange("p t r -> p r t"),
+                in1=b2[s][:].unsqueeze(1).to_broadcast([P, P, PACK]),
+                op=ADD,
+            )
+
+        def quantise_cat(n):
+            cat_codes[n] = quantise(cat_grouped[n], "cat_codes", "cat_scales")
+
+        def stage_2(n, k):
+            codes, scales = cat_codes[n]
+            sums = psum_2.tile([P, D], F32)
+            for s in range(STREAMS):
+                tokens = slice((k * STREAMS + s) * P, (k * STREAMS + s + 1) * P)
+                nc.tensor.matmul_mx(
+                    out=sums[:],
+                    lhsT=codes[:, tokens].bitcast(FP8X4),
+                    lhsT_scale=scales[:, tokens],
+                    rhs=we_codes[:, s, :].bitcast(FP8X4),
+                    rhs_scale=we_scales[:, s, :],
+                    start=(s == 0),
+                    stop=(s == STREAMS - 1),
+                )
+            sums_2[(n, k)] = sums
+
+        def new_norm(n):
+            biased = tail.tile([P, TILES, D], F32)
+            totals = tail.tile([P, TILES], F32)
+            wave[n] = biased
+            square_sums[n] = totals
+
+        def norm_first_half(n, k):
+            nc.vector.tensor_tensor(out=wave[n][:, k, :], in0=sums_2[(n, k)][:], in1=be_all[:], op=ADD)
+            squares = work.tile([P, D], BF16)
+            nc.scalar.activation(
+                out=squares[:], in_=wave[n][:, k, :], func=ACT.Square, accum_out=square_sums[n][:, k : k + 1]
+            )
+
+        def reciprocal_rms(n):
+            factors = tail.tile([P, TILES], F32)
+            nc.scalar.activation(
+                out=factors[:], in_=square_sums[n][:], func=ACT.Abs_reciprocal_sqrt, scale=1.0 / D, bias=eps[:]
+            )
+            inv_rms[n] = factors
+
+        def out_rows(n):
+            return out_dram[n * STEP_TOKENS : (n + 1) * STEP_TOKENS, :].rearrange("(p k) d -> p k d", k=TILES)
+
+        def gain_scale_store(n):
+            with_gain = tail.tile([P, TILES, D], F32)
+            result = tail.tile([P, TILES, D], F32)
+            for k in range(TILES):
+                nc.gpsimd.tensor_tensor(out=with_gain[:, k, :], in0=wave[n][:, k, :], in1=gain_all[:], op=MULT)
+            for k in range(TILES):
+                nc.scalar.activation(out=result[:, k, :], in_=with_gain[:, k, :], func=ACT.Copy, scale=inv_rms[n][:, k : k + 1])
+                nc.sync.dma_start(out=out_rows(n)[:, k, :], in_=result[:, k, :])
+
+        def gain_scale_store_on_vector(n):
+            result = tail.tile([P, TILES, D], F32)
+            for k in range(TILES):
+                nc.vector.scalar_tensor_tensor(
+                    out=result[:, k, :],
+                    in0=wave[n][:, k, :],
+                    scalar=inv_rms[n][:, k : k + 1],
+                    in1=gain_all[:],
+                    op0=MULT,
+                    op1=MULT,
+                )
+                nc.sync.dma_start(out=out_rows(n)[:, k, :], in_=result[:, k, :])
+
+        def is_step(n):
+            return 0 <= n < STEPS
+
+        for i in range(-2, STEPS + 2):
+            if is_step(i + 1):
+                copy_h(i + 1)
+            if i == 0:
+                regroup_we()
+            if is_step(i - 2):
+                new_norm(i - 2)
+            for k in range(TILES):
+                if is_step(i - 2):
+                    norm_first_half(i - 2, k)
+                if is_step(i - 1):
+                    stage_2(i - 1, k)
+            if is_step(i - 2):
+                reciprocal_rms(i - 2)
+            if is_step(i - 2) and i - 2 < STEPS - VECTOR_FINISHES:
+                gain_scale_store(i - 2)
+            if is_step(i + 2):
+                transposes(i + 2)
+            if is_step(i):
+                new_cat(i)
+                for piece in range(PIECES):
+                    bias_and_round(i, piece)
+            if is_step(i + 1):
+                quantise_h(i + 1)
+                for piece in range(PIECES):
+                    stage_1(i + 1, piece)
+            if is_step(i):
+                quantise_cat(i)
+            if i == 0:
+                quantise_we()
+
+        for n in range(STEPS - VECTOR_FINISHES, STEPS):
+            gain_scale_store_on_vector(n)

@@ -22,8 +22,8 @@ TILES = 2
 STEP_TOKENS = TILES * P
 STEPS = TOKENS // STEP_TOKENS
 PIECES = TILES * STREAMS
+SCALAR_PIECE = PIECES - 1
 EPS = 1e-6
-VECTOR_FINISHES = 2
 LOADS_BEFORE_BROADCASTS = 4
 
 FLOPS = 2 * TOKENS * F * D * STREAMS + 2 * TOKENS * (STREAMS * D) * D
@@ -45,14 +45,11 @@ def tile_wavenetworklm_pb_t_kernel(tc, h_r, h_i, w2r, b2r, w2i, b2i, We, be, g_r
         psum_1 = stack.enter_context(tc.psum_pool(name="psum_1", bufs=4))
         psum_2 = stack.enter_context(tc.psum_pool(name="psum_2", bufs=2))
 
-        def load_h(n):
+        def load_h(n, s):
             rows = slice(n * STEP_TOKENS, (n + 1) * STEP_TOKENS)
-            tiles = []
-            for s in range(STREAMS):
-                h_sb = keep.tile([P, TILES * F], BF16, name="h_%d_%d" % (s, n))
-                nc.sync.dma_start(out=h_sb[:], in_=h_dram[s][rows, :].rearrange("(p k) f -> p (k f)", k=TILES))
-                tiles.append(h_sb)
-            return tiles
+            h_sb = keep.tile([P, TILES * F], BF16, name="h_%d_%d" % (s, n))
+            nc.sync.dma_start(out=h_sb[:], in_=h_dram[s][rows, :].rearrange("(p k) f -> p (k f)", k=TILES))
+            h_tiles[(n, s)] = h_sb
 
         def load_w2(s):
             raw = keep.tile([P, PACK, D], BF16, name="w2_raw_%d" % s)
@@ -64,19 +61,21 @@ def tile_wavenetworklm_pb_t_kernel(tc, h_r, h_i, w2r, b2r, w2i, b2i, We, be, g_r
 
         be_all = keep.tile([P, D], BF16)
         gain_all = keep.tile([P, D], BF16)
-        w2_raw = [None, None]
+        w2_raw = []
         h_tiles = {}
-        w2_raw[0] = load_w2(0)
-        h_tiles[0] = load_h(0)
-        w2_raw[1] = load_w2(1)
-        h_tiles[1] = load_h(1)
+        for s in range(STREAMS):
+            w2_raw.append(load_w2(s))
+            load_h(0, s)
+        for s in range(STREAMS):
+            load_h(1, s)
         we_raw = keep.tile([P, STREAMS, PACK, D], BF16)
         nc.sync.dma_start(
             out=we_raw[:].rearrange("p s t d -> p s (t d)"),
             in_=We.rearrange("(s p t) d -> p s (t d)", s=STREAMS, t=PACK),
         )
         for n in range(2, STEPS):
-            h_tiles[n] = load_h(n)
+            for s in range(STREAMS):
+                load_h(n, s)
             if n == LOADS_BEFORE_BROADCASTS:
                 nc.sync.dma_start(out=be_all[:], in_=be.partition_broadcast(P))
                 nc.sync.dma_start(out=gain_all[:], in_=g_rms.partition_broadcast(P))
@@ -95,47 +94,38 @@ def tile_wavenetworklm_pb_t_kernel(tc, h_r, h_i, w2r, b2r, w2i, b2i, We, be, g_r
         w2_codes = []
         w2_scales = []
 
-        def prepare_w2(s):
+        w2_grouped = []
+        for s in range(STREAMS):
             grouped = keep.tile([P, D * PACK], BF16, name="w2_grouped_%d" % s, align_bytes=64)
-            nc.vector.tensor_copy(
-                out=grouped[:].rearrange("q (t c j) -> q t c j", t=PACK, j=PACK),
-                in_=w2_raw[s][:].rearrange("q j (c t) -> q t c j", t=PACK),
-            )
-            return grouped
-
-        def quantise_w2(s, grouped):
             codes = keep.tile([P, D], U32, name="w2_codes_%d" % s, align_bytes=64)
             scales = keep.tile([P, D], U8, name="w2_scales_%d" % s, align_bytes=64)
-            nc.vector.quantize_mx(out=codes[:].bitcast(FP8X4), scales=scales[:], in_=grouped[:])
+            w2_grouped.append(grouped)
             w2_codes.append(codes)
             w2_scales.append(scales)
 
-        for s in range(STREAMS):
-            quantise_w2(s, prepare_w2(s))
+        def regroup_w2(copy, s, first, last):
+            copy(
+                out=w2_grouped[s][:].rearrange("q (t c j) -> q t c j", t=PACK, j=PACK)[:, first:last],
+                in_=w2_raw[s][:].rearrange("q j (c t) -> q t c j", t=PACK)[:, first:last],
+            )
+
+        def quantise_w2(s):
+            nc.vector.quantize_mx(out=w2_codes[s][:].bitcast(FP8X4), scales=w2_scales[s][:], in_=w2_grouped[s][:])
 
         we_grouped = keep.tile([P, STREAMS, D * PACK], BF16, align_bytes=64)
         we_codes = keep.tile([P, STREAMS, D], U32, align_bytes=64)
         we_scales = keep.tile([P, STREAMS, D], U8, align_bytes=64)
 
-        def regroup_we():
-            nc.scalar.copy(
-                out=we_grouped[:, 0, :].rearrange("p (d t) -> p d t", t=PACK),
-                in_=we_raw[:, 0, :, :].rearrange("p t d -> p d t"),
-            )
-            nc.gpsimd.tensor_scalar(
-                out=we_grouped[:, 1, :].rearrange("p (d t) -> p d t", t=PACK),
-                in0=we_raw[:, 1, :, :].rearrange("p t d -> p d t"),
-                scalar1=1.0,
-                scalar2=0.0,
-                op0=MULT,
-                op1=ADD,
+        def regroup_we(copy, s, first, last):
+            columns = slice(first * (D // 8), last * (D // 8))
+            copy(
+                out=we_grouped[:, s, :].rearrange("p (d t) -> p d t", t=PACK)[:, columns],
+                in_=we_raw[:, s, :, :].rearrange("p t d -> p d t")[:, columns],
             )
 
-        def quantise_we():
+        def quantise_we(s):
             nc.vector.quantize_mx(
-                out=we_codes[:].rearrange("p s d -> p (s d)").bitcast(FP8X4),
-                scales=we_scales[:].rearrange("p s d -> p (s d)"),
-                in_=we_grouped[:].rearrange("p s x -> p (s x)"),
+                out=we_codes[:, s, :].bitcast(FP8X4), scales=we_scales[:, s, :], in_=we_grouped[:, s, :]
             )
 
         h_words = {}
@@ -144,45 +134,49 @@ def tile_wavenetworklm_pb_t_kernel(tc, h_r, h_i, w2r, b2r, w2i, b2i, We, be, g_r
         sums_1 = {}
         cat_grouped = {}
         cat_codes = {}
+        by_feature = {}
         sums_2 = {}
         wave = {}
         square_sums = {}
         inv_rms = {}
 
-        def transposes(n):
+        def transposes(n, s):
+            words = psum_t.tile([P, TILES, 2, P], F32)
+            source = h_tiles[(n, s)][:].bitcast(F32)
             for k in range(TILES):
-                words = psum_t.tile([P, STREAMS, 2, P], F32)
-                for s in range(STREAMS):
-                    source = h_tiles[n][s][:].bitcast(F32)
-                    for u in range(2):
-                        token = slice(k * (F // 2) + u, (k + 1) * (F // 2), 2)
-                        nc.tensor.transpose(words[:, s, u, :], source[:, token], identity[:])
-                h_words[(n, k)] = words
+                for u in range(2):
+                    token = slice(k * (F // 2) + u, (k + 1) * (F // 2), 2)
+                    nc.tensor.transpose(words[:, k, u, :], source[:, token], identity[:])
+            h_words[(n, s)] = words
 
-        def copy_h(n):
-            grouped = work.tile([P, PIECES * P * PACK], BF16, align_bytes=64)
-            grouped_words = grouped[:].bitcast(F32)
-            width = STREAMS * P * 2
-            for k in range(TILES):
-                nc.scalar.copy(
-                    out=grouped_words[:, k * width : (k + 1) * width].rearrange("p (s r u) -> p s r u", s=STREAMS, u=2),
-                    in_=h_words[(n, k)][:].rearrange("p s u r -> p s r u"),
-                )
+        def new_h(n):
+            grouped = work.tile([P, PIECES * P * PACK], BF16, name="h_grouped", align_bytes=64)
+            codes = work.tile([P, PIECES * P], U32, name="h_codes", align_bytes=64)
+            scales = work.tile([P, PIECES * P], U8, name="h_scales", align_bytes=64)
             h_grouped[n] = grouped
+            h_codes[n] = (codes, scales)
 
-        def quantise(grouped, codes_name, scales_name):
-            codes = work.tile([P, PIECES * P], U32, name=codes_name, align_bytes=64)
-            scales = work.tile([P, PIECES * P], U8, name=scales_name, align_bytes=64)
-            nc.vector.quantize_mx(out=codes[:].bitcast(FP8X4), scales=scales[:], in_=grouped[:])
-            return codes, scales
+        def copy_h(n, s):
+            width = TILES * P * 2
+            nc.scalar.copy(
+                out=h_grouped[n][:].bitcast(F32)[:, s * width : (s + 1) * width].rearrange("p (k r u) -> p k r u", k=TILES, u=2),
+                in_=h_words[(n, s)][:].rearrange("p k u r -> p k r u"),
+            )
 
-        def quantise_h(n):
-            h_codes[n] = quantise(h_grouped[n], "h_codes", "h_scales")
+        def quantise_h(n, first, last):
+            codes, scales = h_codes[n]
+            words = slice(first * TILES * P, last * TILES * P)
+            nc.vector.quantize_mx(
+                out=codes[:, words].bitcast(FP8X4),
+                scales=scales[:, words],
+                in_=h_grouped[n][:, first * TILES * P * PACK : last * TILES * P * PACK],
+            )
 
         def stage_1(n, piece):
-            s = piece % STREAMS
+            k, s = divmod(piece, STREAMS)
             codes, scales = h_codes[n]
-            tokens = slice(piece * P, (piece + 1) * P)
+            first = (s * TILES + k) * P
+            tokens = slice(first, first + P)
             sums = psum_1.tile([P, PACK, P], F32)
             for t in range(PACK):
                 columns = slice(t * P, (t + 1) * P)
@@ -199,7 +193,10 @@ def tile_wavenetworklm_pb_t_kernel(tc, h_r, h_i, w2r, b2r, w2i, b2i, We, be, g_r
 
         def new_cat(n):
             cat = work.tile([P, PIECES * P * PACK], BF16, align_bytes=64)
+            codes = work.tile([P, PIECES * P], U32, name="cat_codes", align_bytes=64)
+            scales = work.tile([P, PIECES * P], U8, name="cat_scales", align_bytes=64)
             cat_grouped[n] = cat
+            cat_codes[n] = (codes, scales)
 
         def bias_and_round(n, piece):
             s = piece % STREAMS
@@ -211,8 +208,32 @@ def tile_wavenetworklm_pb_t_kernel(tc, h_r, h_i, w2r, b2r, w2i, b2i, We, be, g_r
                 op=ADD,
             )
 
-        def quantise_cat(n):
-            cat_codes[n] = quantise(cat_grouped[n], "cat_codes", "cat_scales")
+        def bias_and_round_on_scalar(n):
+            rounded = work.tile([P, PACK, P], BF16)
+            for t in range(PACK):
+                nc.scalar.activation(
+                    out=rounded[:, t, :],
+                    in_=sums_1[(n, SCALAR_PIECE)][:, t, :],
+                    func=ACT.Identity,
+                    bias=b2[SCALAR_PIECE % STREAMS][:, t : t + 1],
+                )
+            by_feature[n] = rounded
+
+        def interleave(n):
+            width = P * PACK
+            nc.vector.tensor_copy(
+                out=cat_grouped[n][:, SCALAR_PIECE * width : (SCALAR_PIECE + 1) * width].rearrange("p (r t) -> p r t", t=PACK),
+                in_=by_feature[n][:].rearrange("p t r -> p r t"),
+            )
+
+        def quantise_cat(n, first, last):
+            codes, scales = cat_codes[n]
+            words = slice(first * STREAMS * P, last * STREAMS * P)
+            nc.vector.quantize_mx(
+                out=codes[:, words].bitcast(FP8X4),
+                scales=scales[:, words],
+                in_=cat_grouped[n][:, first * STREAMS * P * PACK : last * STREAMS * P * PACK],
+            )
 
         def stage_2(n, k):
             codes, scales = cat_codes[n]
@@ -233,8 +254,10 @@ def tile_wavenetworklm_pb_t_kernel(tc, h_r, h_i, w2r, b2r, w2i, b2i, We, be, g_r
         def new_norm(n):
             biased = tail.tile([P, TILES, D], F32)
             totals = tail.tile([P, TILES], F32)
+            factors = tail.tile([P, TILES], F32)
             wave[n] = biased
             square_sums[n] = totals
+            inv_rms[n] = factors
 
         def norm_first_half(n, k):
             nc.vector.tensor_tensor(out=wave[n][:, k, :], in0=sums_2[(n, k)][:], in1=be_all[:], op=ADD)
@@ -243,12 +266,14 @@ def tile_wavenetworklm_pb_t_kernel(tc, h_r, h_i, w2r, b2r, w2i, b2i, We, be, g_r
                 out=squares[:], in_=wave[n][:, k, :], func=ACT.Square, accum_out=square_sums[n][:, k : k + 1]
             )
 
-        def reciprocal_rms(n):
-            factors = tail.tile([P, TILES], F32)
+        def reciprocal_rms(n, first, last):
             nc.scalar.activation(
-                out=factors[:], in_=square_sums[n][:], func=ACT.Abs_reciprocal_sqrt, scale=1.0 / D, bias=eps[:]
+                out=inv_rms[n][:, first:last],
+                in_=square_sums[n][:, first:last],
+                func=ACT.Abs_reciprocal_sqrt,
+                scale=1.0 / D,
+                bias=eps[:],
             )
-            inv_rms[n] = factors
 
         def out_rows(n):
             return out_dram[n * STEP_TOKENS : (n + 1) * STEP_TOKENS, :].rearrange("(p k) d -> p k d", k=TILES)
@@ -262,52 +287,120 @@ def tile_wavenetworklm_pb_t_kernel(tc, h_r, h_i, w2r, b2r, w2i, b2i, We, be, g_r
                 nc.scalar.activation(out=result[:, k, :], in_=with_gain[:, k, :], func=ACT.Copy, scale=inv_rms[n][:, k : k + 1])
                 nc.sync.dma_start(out=out_rows(n)[:, k, :], in_=result[:, k, :])
 
-        def gain_scale_store_on_vector(n):
-            result = tail.tile([P, TILES, D], F32)
-            for k in range(TILES):
-                nc.vector.scalar_tensor_tensor(
-                    out=result[:, k, :],
-                    in0=wave[n][:, k, :],
-                    scalar=inv_rms[n][:, k : k + 1],
-                    in1=gain_all[:],
-                    op0=MULT,
-                    op1=MULT,
-                )
-                nc.sync.dma_start(out=out_rows(n)[:, k, :], in_=result[:, k, :])
+        def gain_scale_store_on_vector(n, k):
+            result = tail.tile([P, D], F32, name="last_result", bufs=2 * TILES)
+            nc.vector.scalar_tensor_tensor(
+                out=result[:],
+                in0=wave[n][:, k, :],
+                scalar=inv_rms[n][:, k : k + 1],
+                in1=gain_all[:],
+                op0=MULT,
+                op1=MULT,
+            )
+            nc.sync.dma_start(out=out_rows(n)[:, k, :], in_=result[:])
 
-        def is_step(n):
-            return 0 <= n < STEPS
+        new_h(0)
+        new_h(1)
+        new_cat(0)
+        transposes(0, 0)
+        copy_h(0, 0)
+        regroup_w2(nc.vector.tensor_copy, 0, 0, PACK)
+        quantise_w2(0)
+        regroup_w2(nc.scalar.copy, 1, 3, PACK)
+        regroup_w2(nc.vector.tensor_copy, 1, 0, 1)
+        quantise_h(0, 0, 1)
+        regroup_w2(nc.vector.tensor_copy, 1, 1, 3)
+        transposes(0, 1)
+        copy_h(0, 1)
+        for k in range(TILES):
+            stage_1(0, k * STREAMS)
+        quantise_w2(1)
+        quantise_h(0, 1, STREAMS)
+        for k in range(TILES):
+            bias_and_round(0, k * STREAMS)
+        for k in range(TILES):
+            stage_1(0, k * STREAMS + 1)
+        for s in range(STREAMS):
+            transposes(1, s)
+            copy_h(1, s)
+        for k in range(TILES):
+            bias_and_round(0, k * STREAMS + 1)
+        regroup_we(nc.vector.tensor_copy, 1, 0, 8)
+        regroup_we(nc.scalar.copy, 0, 0, 6)
+        quantise_h(1, 0, STREAMS)
+        for piece in range(PIECES):
+            stage_1(1, piece)
+        quantise_cat(0, 0, TILES)
+        new_h(2)
+        for s in range(STREAMS):
+            transposes(2, s)
+            copy_h(2, s)
+        regroup_we(nc.scalar.copy, 0, 6, 8)
 
-        for i in range(-2, STEPS + 2):
-            if is_step(i + 1):
-                copy_h(i + 1)
-            if i == 0:
-                regroup_we()
-            if is_step(i - 2):
-                new_norm(i - 2)
+        new_cat(1)
+        for piece in range(PIECES):
+            bias_and_round(1, piece)
+        quantise_h(2, 0, STREAMS)
+        quantise_cat(1, 0, TILES)
+        for s in range(STREAMS):
+            transposes(3, s)
+        for s in range(STREAMS):
+            quantise_we(s)
+        for k in range(TILES):
+            stage_2(0, k)
+        for piece in range(PIECES):
+            stage_1(2, piece)
+
+        for i in range(2, STEPS - 1):
+            new_h(i + 1)
+            for s in range(STREAMS):
+                copy_h(i + 1, s)
+            bias_and_round_on_scalar(i)
+            new_norm(i - 2)
             for k in range(TILES):
-                if is_step(i - 2):
-                    norm_first_half(i - 2, k)
-                if is_step(i - 1):
-                    stage_2(i - 1, k)
-            if is_step(i - 2):
-                reciprocal_rms(i - 2)
-            if is_step(i - 2) and i - 2 < STEPS - VECTOR_FINISHES:
-                gain_scale_store(i - 2)
-            if is_step(i + 2):
-                transposes(i + 2)
-            if is_step(i):
-                new_cat(i)
-                for piece in range(PIECES):
+                norm_first_half(i - 2, k)
+                stage_2(i - 1, k)
+            reciprocal_rms(i - 2, 0, TILES)
+            gain_scale_store(i - 2)
+            if i + 2 < STEPS:
+                for s in range(STREAMS):
+                    transposes(i + 2, s)
+            new_cat(i)
+            for piece in range(PIECES):
+                if piece != SCALAR_PIECE:
                     bias_and_round(i, piece)
-            if is_step(i + 1):
-                quantise_h(i + 1)
-                for piece in range(PIECES):
-                    stage_1(i + 1, piece)
-            if is_step(i):
-                quantise_cat(i)
-            if i == 0:
-                quantise_we()
+            interleave(i)
+            quantise_h(i + 1, 0, STREAMS)
+            for piece in range(PIECES):
+                stage_1(i + 1, piece)
+            quantise_cat(i, 0, TILES)
 
-        for n in range(STEPS - VECTOR_FINISHES, STEPS):
-            gain_scale_store_on_vector(n)
+        last = STEPS - 1
+        for n in range(last - 2, last + 1):
+            new_norm(n)
+        new_cat(last)
+        bias_and_round_on_scalar(last)
+        for k in range(TILES):
+            norm_first_half(last - 2, k)
+            stage_2(last - 1, k)
+        reciprocal_rms(last - 2, 0, TILES)
+        gain_scale_store(last - 2)
+        for s in range(STREAMS):
+            bias_and_round(last, s)
+        bias_and_round(last, STREAMS)
+        quantise_cat(last, 0, 1)
+        norm_first_half(last - 1, 0)
+        stage_2(last, 0)
+        interleave(last)
+        norm_first_half(last - 1, 1)
+        reciprocal_rms(last - 1, 0, TILES)
+        quantise_cat(last, 1, TILES)
+        stage_2(last, 1)
+        norm_first_half(last, 0)
+        reciprocal_rms(last, 0, 1)
+        gain_scale_store_on_vector(last - 1, 0)
+        norm_first_half(last, 1)
+        reciprocal_rms(last, 1, TILES)
+        gain_scale_store_on_vector(last - 1, 1)
+        for k in range(TILES):
+            gain_scale_store_on_vector(last, k)

@@ -40,7 +40,8 @@ def tile_wavenetworklm_pb_t_kernel(tc, h_r, h_i, w2r, b2r, w2i, b2i, We, be, g_r
         stack.enter_context(tc.manual_schedule())
         keep = stack.enter_context(tc.tile_pool(name="keep", bufs=1))
         work = stack.enter_context(tc.tile_pool(name="work", bufs=2))
-        tail = stack.enter_context(tc.tile_pool(name="tail", bufs=3))
+        tail = stack.enter_context(tc.tile_pool(name="tail", bufs=4))
+        turns = stack.enter_context(tc.tile_pool(name="turns", bufs=3))
         psum_t = stack.enter_context(tc.psum_pool(name="psum_t", bufs=2))
         psum_1 = stack.enter_context(tc.psum_pool(name="psum_1", bufs=4))
         psum_2 = stack.enter_context(tc.psum_pool(name="psum_2", bufs=2))
@@ -84,6 +85,8 @@ def tile_wavenetworklm_pb_t_kernel(tc, h_r, h_i, w2r, b2r, w2i, b2i, We, be, g_r
         make_identity(nc, identity[:])
         eps = keep.tile([P, 1], F32)
         nc.vector.memset(eps[:], EPS)
+        unused = keep.tile([P, 1], F32)
+        nc.scalar.activation(out=unused[:], in_=eps[:], func=ACT.Abs_reciprocal_sqrt)
 
         b2 = []
         for s in range(STREAMS):
@@ -192,7 +195,7 @@ def tile_wavenetworklm_pb_t_kernel(tc, h_r, h_i, w2r, b2r, w2i, b2i, We, be, g_r
             sums_1[(n, piece)] = sums
 
         def new_cat(n):
-            cat = work.tile([P, PIECES * P * PACK], BF16, align_bytes=64)
+            cat = turns.tile([P, PIECES * P * PACK], BF16, name="turn", align_bytes=64)
             codes = work.tile([P, PIECES * P], U32, name="cat_codes", align_bytes=64)
             scales = work.tile([P, PIECES * P], U8, name="cat_scales", align_bytes=64)
             cat_grouped[n] = cat
@@ -278,17 +281,21 @@ def tile_wavenetworklm_pb_t_kernel(tc, h_r, h_i, w2r, b2r, w2i, b2i, We, be, g_r
         def out_rows(n):
             return out_dram[n * STEP_TOKENS : (n + 1) * STEP_TOKENS, :].rearrange("(p k) d -> p k d", k=TILES)
 
-        def gain_scale_store(n):
-            with_gain = tail.tile([P, TILES, D], F32)
+        def gain_scale_store(n, first, last):
+            with_gain = turns.tile([P, TILES, D], F32, name="turn", align_bytes=64)
             result = tail.tile([P, TILES, D], F32)
-            for k in range(TILES):
-                nc.gpsimd.tensor_tensor(out=with_gain[:, k, :], in0=wave[n][:, k, :], in1=gain_all[:], op=MULT)
-            for k in range(TILES):
+            nc.gpsimd.tensor_tensor(
+                out=with_gain[:, first:last, :],
+                in0=wave[n][:, first:last, :],
+                in1=gain_all[:].unsqueeze(1).to_broadcast([P, last - first, D]),
+                op=MULT,
+            )
+            for k in range(first, last):
                 nc.scalar.activation(out=result[:, k, :], in_=with_gain[:, k, :], func=ACT.Copy, scale=inv_rms[n][:, k : k + 1])
                 nc.sync.dma_start(out=out_rows(n)[:, k, :], in_=result[:, k, :])
 
         def gain_scale_store_on_vector(n, k):
-            result = tail.tile([P, D], F32, name="last_result", bufs=2 * TILES)
+            result = tail.tile([P, D], F32, name="last_result", bufs=3 * TILES)
             nc.vector.scalar_tensor_tensor(
                 out=result[:],
                 in0=wave[n][:, k, :],
@@ -353,6 +360,7 @@ def tile_wavenetworklm_pb_t_kernel(tc, h_r, h_i, w2r, b2r, w2i, b2i, We, be, g_r
 
         for i in range(2, STEPS - 1):
             new_h(i + 1)
+            new_cat(i)
             for s in range(STREAMS):
                 copy_h(i + 1, s)
             bias_and_round_on_scalar(i)
@@ -361,11 +369,11 @@ def tile_wavenetworklm_pb_t_kernel(tc, h_r, h_i, w2r, b2r, w2i, b2i, We, be, g_r
                 norm_first_half(i - 2, k)
                 stage_2(i - 1, k)
             reciprocal_rms(i - 2, 0, TILES)
-            gain_scale_store(i - 2)
+            if i > 2:
+                gain_scale_store(i - 3, 0, TILES)
             if i + 2 < STEPS:
                 for s in range(STREAMS):
                     transposes(i + 2, s)
-            new_cat(i)
             for piece in range(PIECES):
                 if piece != SCALAR_PIECE:
                     bias_and_round(i, piece)
@@ -376,31 +384,27 @@ def tile_wavenetworklm_pb_t_kernel(tc, h_r, h_i, w2r, b2r, w2i, b2i, We, be, g_r
             quantise_cat(i, 0, TILES)
 
         last = STEPS - 1
+        new_cat(last)
         for n in range(last - 2, last + 1):
             new_norm(n)
-        new_cat(last)
-        bias_and_round_on_scalar(last)
         for k in range(TILES):
             norm_first_half(last - 2, k)
             stage_2(last - 1, k)
         reciprocal_rms(last - 2, 0, TILES)
-        gain_scale_store(last - 2)
-        for s in range(STREAMS):
-            bias_and_round(last, s)
-        bias_and_round(last, STREAMS)
-        quantise_cat(last, 0, 1)
-        norm_first_half(last - 1, 0)
-        stage_2(last, 0)
-        interleave(last)
-        norm_first_half(last - 1, 1)
-        reciprocal_rms(last - 1, 0, TILES)
-        quantise_cat(last, 1, TILES)
-        stage_2(last, 1)
-        norm_first_half(last, 0)
-        reciprocal_rms(last, 0, 1)
-        gain_scale_store_on_vector(last - 1, 0)
-        norm_first_half(last, 1)
-        reciprocal_rms(last, 1, TILES)
-        gain_scale_store_on_vector(last - 1, 1)
+        gain_scale_store(last - 3, 0, TILES)
+        for piece in range(PIECES):
+            bias_and_round(last, piece)
         for k in range(TILES):
-            gain_scale_store_on_vector(last, k)
+            norm_first_half(last - 1, k)
+        gain_scale_store(last - 2, 0, 1)
+        reciprocal_rms(last - 1, 0, TILES)
+        quantise_cat(last, 0, TILES)
+        for k in range(TILES):
+            stage_2(last, k)
+        gain_scale_store_on_vector(last - 2, 1)
+        for k in range(TILES):
+            norm_first_half(last, k)
+            reciprocal_rms(last, k, k + 1)
+        for n in range(last - 1, last + 1):
+            for k in range(TILES):
+                gain_scale_store_on_vector(n, k)

@@ -24,7 +24,6 @@ STEPS = TOKENS // STEP_TOKENS
 PIECES = TILES * STREAMS
 SCALAR_PIECE = PIECES - 1
 EPS = 1e-6
-LOADS_BEFORE_BROADCASTS = 4
 
 FLOPS = 2 * TOKENS * F * D * STREAMS + 2 * TOKENS * (STREAMS * D) * D
 
@@ -41,7 +40,7 @@ def tile_wavenetworklm_pb_t_kernel(tc, h_r, h_i, w2r, b2r, w2i, b2i, We, be, g_r
         keep = stack.enter_context(tc.tile_pool(name="keep", bufs=1))
         work = stack.enter_context(tc.tile_pool(name="work", bufs=2))
         tail = stack.enter_context(tc.tile_pool(name="tail", bufs=4))
-        turns = stack.enter_context(tc.tile_pool(name="turns", bufs=3))
+        turns = stack.enter_context(tc.tile_pool(name="turns", bufs=2))
         psum_t = stack.enter_context(tc.psum_pool(name="psum_t", bufs=2))
         psum_1 = stack.enter_context(tc.psum_pool(name="psum_1", bufs=4))
         psum_2 = stack.enter_context(tc.psum_pool(name="psum_2", bufs=2))
@@ -67,19 +66,19 @@ def tile_wavenetworklm_pb_t_kernel(tc, h_r, h_i, w2r, b2r, w2i, b2i, We, be, g_r
         for s in range(STREAMS):
             w2_raw.append(load_w2(s))
             load_h(0, s)
+        we_raw = []
         for s in range(STREAMS):
-            load_h(1, s)
-        we_raw = keep.tile([P, STREAMS, PACK, D], BF16)
-        nc.sync.dma_start(
-            out=we_raw[:].rearrange("p s t d -> p s (t d)"),
-            in_=We.rearrange("(s p t) d -> p s (t d)", s=STREAMS, t=PACK),
-        )
-        for n in range(2, STEPS):
+            half = keep.tile([P, PACK, D], BF16, name="we_raw_%d" % s)
+            nc.sync.dma_start(
+                out=half[:].rearrange("p t d -> p (t d)"),
+                in_=We[s * D : (s + 1) * D, :].rearrange("(p t) d -> p (t d)", t=PACK),
+            )
+            we_raw.append(half)
+            for stream in range(STREAMS):
+                load_h(1 + s, stream)
+        for n in range(3, STEPS):
             for s in range(STREAMS):
                 load_h(n, s)
-            if n == LOADS_BEFORE_BROADCASTS:
-                nc.sync.dma_start(out=be_all[:], in_=be.partition_broadcast(P))
-                nc.sync.dma_start(out=gain_all[:], in_=g_rms.partition_broadcast(P))
 
         identity = keep.tile([P, P], F32)
         make_identity(nc, identity[:])
@@ -88,11 +87,24 @@ def tile_wavenetworklm_pb_t_kernel(tc, h_r, h_i, w2r, b2r, w2i, b2i, We, be, g_r
         unused = keep.tile([P, 1], F32)
         nc.scalar.activation(out=unused[:], in_=eps[:], func=ACT.Abs_reciprocal_sqrt)
 
+        rows = keep.tile([P, 2, D], BF16)
+        ones = keep.tile([P, P], BF16)
+        nc.vector.memset(rows[:].rearrange("p v d -> p (v d)").bitcast(U32), 0)
+        nc.vector.memset(ones[:], 1.0)
+
         b2 = []
         for s in range(STREAMS):
             b2_sb = keep.tile([P, PACK], BF16, name="b2_%d" % s)
             nc.scalar.dma_start(out=b2_sb[:], in_=b2_dram[s].rearrange("(p t) -> p t", t=PACK))
             b2.append(b2_sb)
+        for v, vector in enumerate((be, g_rms)):
+            nc.scalar.dma_start(out=rows[0:1, v, :], in_=vector.unsqueeze(0))
+
+        def spread_rows():
+            for v, spread in enumerate((be_all, gain_all)):
+                sums = psum_2.tile([P, D], F32)
+                nc.tensor.matmul(out=sums[:], lhsT=ones[:], rhs=rows[:, v, :], start=True, stop=True)
+                nc.scalar.copy(out=spread[:], in_=sums[:])
 
         w2_codes = []
         w2_scales = []
@@ -123,7 +135,7 @@ def tile_wavenetworklm_pb_t_kernel(tc, h_r, h_i, w2r, b2r, w2i, b2i, We, be, g_r
             columns = slice(first * (D // 8), last * (D // 8))
             copy(
                 out=we_grouped[:, s, :].rearrange("p (d t) -> p d t", t=PACK)[:, columns],
-                in_=we_raw[:, s, :, :].rearrange("p t d -> p d t")[:, columns],
+                in_=we_raw[s][:].rearrange("p t d -> p d t")[:, columns],
             )
 
         def quantise_we(s):
@@ -310,8 +322,9 @@ def tile_wavenetworklm_pb_t_kernel(tc, h_r, h_i, w2r, b2r, w2i, b2i, We, be, g_r
         new_h(1)
         new_cat(0)
         transposes(0, 0)
+        regroup_w2(nc.scalar.copy, 0, 2, PACK)
+        regroup_w2(nc.vector.tensor_copy, 0, 0, 2)
         copy_h(0, 0)
-        regroup_w2(nc.vector.tensor_copy, 0, 0, PACK)
         quantise_w2(0)
         regroup_w2(nc.scalar.copy, 1, 3, PACK)
         regroup_w2(nc.vector.tensor_copy, 1, 0, 1)
@@ -323,6 +336,7 @@ def tile_wavenetworklm_pb_t_kernel(tc, h_r, h_i, w2r, b2r, w2i, b2i, We, be, g_r
             stage_1(0, k * STREAMS)
         quantise_w2(1)
         quantise_h(0, 1, STREAMS)
+        regroup_we(nc.scalar.copy, 0, 0, 4)
         for k in range(TILES):
             bias_and_round(0, k * STREAMS)
         for k in range(TILES):
@@ -332,27 +346,29 @@ def tile_wavenetworklm_pb_t_kernel(tc, h_r, h_i, w2r, b2r, w2i, b2i, We, be, g_r
             copy_h(1, s)
         for k in range(TILES):
             bias_and_round(0, k * STREAMS + 1)
-        regroup_we(nc.vector.tensor_copy, 1, 0, 8)
-        regroup_we(nc.scalar.copy, 0, 0, 6)
+        regroup_we(nc.vector.tensor_copy, 1, 0, 6)
+        regroup_we(nc.scalar.copy, 0, 4, 8)
+        regroup_we(nc.scalar.copy, 1, 6, 8)
         quantise_h(1, 0, STREAMS)
+        new_h(2)
+        transposes(2, 0)
+        transposes(2, 1)
         for piece in range(PIECES):
             stage_1(1, piece)
         quantise_cat(0, 0, TILES)
-        new_h(2)
         for s in range(STREAMS):
-            transposes(2, s)
             copy_h(2, s)
-        regroup_we(nc.scalar.copy, 0, 6, 8)
 
         new_cat(1)
         for piece in range(PIECES):
             bias_and_round(1, piece)
+        spread_rows()
         quantise_h(2, 0, STREAMS)
+        for s in range(STREAMS):
+            quantise_we(s)
         quantise_cat(1, 0, TILES)
         for s in range(STREAMS):
             transposes(3, s)
-        for s in range(STREAMS):
-            quantise_we(s)
         for k in range(TILES):
             stage_2(0, k)
         for piece in range(PIECES):

@@ -60,7 +60,7 @@ def tile_wavenetworklm_pb_t_kernel(tc, h_r, h_i, w2r, b2r, w2i, b2i, We, be, g_r
             return raw
 
         be_all = keep.tile([P, D], BF16)
-        gain_all = keep.tile([P, D], BF16)
+        gain_all = keep.tile([P, TILES, D], BF16)
         w2_raw = []
         h_tiles = {}
         for s in range(STREAMS):
@@ -101,10 +101,11 @@ def tile_wavenetworklm_pb_t_kernel(tc, h_r, h_i, w2r, b2r, w2i, b2i, We, be, g_r
             nc.scalar.dma_start(out=rows[0:1, v, :], in_=vector.unsqueeze(0))
 
         def spread_rows():
-            for v, spread in enumerate((be_all, gain_all)):
+            for v, copies in enumerate(((be_all[:],), [gain_all[:, k, :] for k in range(TILES)])):
                 sums = psum_2.tile([P, D], F32)
                 nc.tensor.matmul(out=sums[:], lhsT=ones[:], rhs=rows[:, v, :], start=True, stop=True)
-                nc.scalar.copy(out=spread[:], in_=sums[:])
+                for spread in copies:
+                    nc.scalar.copy(out=spread, in_=sums[:])
 
         w2_codes = []
         w2_scales = []
@@ -299,7 +300,7 @@ def tile_wavenetworklm_pb_t_kernel(tc, h_r, h_i, w2r, b2r, w2i, b2i, We, be, g_r
             nc.gpsimd.tensor_tensor(
                 out=with_gain[:, first:last, :],
                 in0=wave[n][:, first:last, :],
-                in1=gain_all[:].unsqueeze(1).to_broadcast([P, last - first, D]),
+                in1=gain_all[:, first:last, :],
                 op=MULT,
             )
             for k in range(first, last):
@@ -312,7 +313,7 @@ def tile_wavenetworklm_pb_t_kernel(tc, h_r, h_i, w2r, b2r, w2i, b2i, We, be, g_r
                 out=result[:],
                 in0=wave[n][:, k, :],
                 scalar=inv_rms[n][:, k : k + 1],
-                in1=gain_all[:],
+                in1=gain_all[:, k, :],
                 op0=MULT,
                 op1=MULT,
             )

@@ -22,7 +22,6 @@ TILES = 2
 STEP_TOKENS = TILES * P
 STEPS = TOKENS // STEP_TOKENS
 PIECES = TILES * STREAMS
-SCALAR_PIECE = PIECES - 1
 EPS = 1e-6
 
 FLOPS = 2 * TOKENS * F * D * STREAMS + 2 * TOKENS * (STREAMS * D) * D
@@ -40,7 +39,6 @@ def tile_wavenetworklm_pb_t_kernel(tc, h_r, h_i, w2r, b2r, w2i, b2i, We, be, g_r
         keep = stack.enter_context(tc.tile_pool(name="keep", bufs=1))
         work = stack.enter_context(tc.tile_pool(name="work", bufs=2))
         tail = stack.enter_context(tc.tile_pool(name="tail", bufs=4))
-        turns = stack.enter_context(tc.tile_pool(name="turns", bufs=2))
         psum_t = stack.enter_context(tc.psum_pool(name="psum_t", bufs=2))
         psum_1 = stack.enter_context(tc.psum_pool(name="psum_1", bufs=4))
         psum_2 = stack.enter_context(tc.psum_pool(name="psum_2", bufs=2))
@@ -150,7 +148,6 @@ def tile_wavenetworklm_pb_t_kernel(tc, h_r, h_i, w2r, b2r, w2i, b2i, We, be, g_r
         sums_1 = {}
         cat_grouped = {}
         cat_codes = {}
-        by_feature = {}
         sums_2 = {}
         wave = {}
         square_sums = {}
@@ -166,7 +163,7 @@ def tile_wavenetworklm_pb_t_kernel(tc, h_r, h_i, w2r, b2r, w2i, b2i, We, be, g_r
             h_words[(n, s)] = words
 
         def new_h(n):
-            grouped = work.tile([P, PIECES * P * PACK], BF16, name="h_grouped", align_bytes=64)
+            grouped = work.tile([P, PIECES * P * PACK], BF16, name="h_grouped", bufs=3, align_bytes=64)
             codes = work.tile([P, PIECES * P], U32, name="h_codes", align_bytes=64)
             scales = work.tile([P, PIECES * P], U8, name="h_scales", align_bytes=64)
             h_grouped[n] = grouped
@@ -208,7 +205,7 @@ def tile_wavenetworklm_pb_t_kernel(tc, h_r, h_i, w2r, b2r, w2i, b2i, We, be, g_r
             sums_1[(n, piece)] = sums
 
         def new_cat(n):
-            cat = turns.tile([P, PIECES * P * PACK], BF16, name="turn", align_bytes=64)
+            cat = work.tile([P, PIECES * P * PACK], BF16, align_bytes=64)
             codes = work.tile([P, PIECES * P], U32, name="cat_codes", align_bytes=64)
             scales = work.tile([P, PIECES * P], U8, name="cat_scales", align_bytes=64)
             cat_grouped[n] = cat
@@ -222,24 +219,6 @@ def tile_wavenetworklm_pb_t_kernel(tc, h_r, h_i, w2r, b2r, w2i, b2i, We, be, g_r
                 in0=sums_1[(n, piece)][:].rearrange("p t r -> p r t"),
                 in1=b2[s][:].unsqueeze(1).to_broadcast([P, P, PACK]),
                 op=ADD,
-            )
-
-        def bias_and_round_on_scalar(n):
-            rounded = work.tile([P, PACK, P], BF16)
-            for t in range(PACK):
-                nc.scalar.activation(
-                    out=rounded[:, t, :],
-                    in_=sums_1[(n, SCALAR_PIECE)][:, t, :],
-                    func=ACT.Identity,
-                    bias=b2[SCALAR_PIECE % STREAMS][:, t : t + 1],
-                )
-            by_feature[n] = rounded
-
-        def interleave(n):
-            width = P * PACK
-            nc.vector.tensor_copy(
-                out=cat_grouped[n][:, SCALAR_PIECE * width : (SCALAR_PIECE + 1) * width].rearrange("p (r t) -> p r t", t=PACK),
-                in_=by_feature[n][:].rearrange("p t r -> p r t"),
             )
 
         def quantise_cat(n, first, last):
@@ -294,8 +273,8 @@ def tile_wavenetworklm_pb_t_kernel(tc, h_r, h_i, w2r, b2r, w2i, b2i, We, be, g_r
         def out_rows(n):
             return out_dram[n * STEP_TOKENS : (n + 1) * STEP_TOKENS, :].rearrange("(p k) d -> p k d", k=TILES)
 
-        def gain_scale_store(n, first, last):
-            with_gain = turns.tile([P, TILES, D], F32, name="turn", align_bytes=64)
+        def gain_scale_store(n, spent, first, last):
+            with_gain = h_grouped[spent][:].bitcast(F32).rearrange("p (k d) -> p k d", k=TILES)
             result = tail.tile([P, TILES, D], F32)
             nc.gpsimd.tensor_tensor(
                 out=with_gain[:, first:last, :],
@@ -304,7 +283,9 @@ def tile_wavenetworklm_pb_t_kernel(tc, h_r, h_i, w2r, b2r, w2i, b2i, We, be, g_r
                 op=MULT,
             )
             for k in range(first, last):
-                nc.scalar.activation(out=result[:, k, :], in_=with_gain[:, k, :], func=ACT.Copy, scale=inv_rms[n][:, k : k + 1])
+                nc.scalar.activation(
+                    out=result[:, k, :], in_=with_gain[:, k, :], func=ACT.Copy, scale=inv_rms[n][:, k : k + 1]
+                )
                 nc.sync.dma_start(out=out_rows(n)[:, k, :], in_=result[:, k, :])
 
         def gain_scale_store_on_vector(n, k):
@@ -380,21 +361,18 @@ def tile_wavenetworklm_pb_t_kernel(tc, h_r, h_i, w2r, b2r, w2i, b2i, We, be, g_r
             new_cat(i)
             for s in range(STREAMS):
                 copy_h(i + 1, s)
-            bias_and_round_on_scalar(i)
             new_norm(i - 2)
             for k in range(TILES):
                 norm_first_half(i - 2, k)
                 stage_2(i - 1, k)
             reciprocal_rms(i - 2, 0, TILES)
             if i > 2:
-                gain_scale_store(i - 3, 0, TILES)
+                gain_scale_store(i - 3, i, 0, TILES)
             if i + 2 < STEPS:
                 for s in range(STREAMS):
                     transposes(i + 2, s)
             for piece in range(PIECES):
-                if piece != SCALAR_PIECE:
-                    bias_and_round(i, piece)
-            interleave(i)
+                bias_and_round(i, piece)
             quantise_h(i + 1, 0, STREAMS)
             for piece in range(PIECES):
                 stage_1(i + 1, piece)
@@ -408,12 +386,12 @@ def tile_wavenetworklm_pb_t_kernel(tc, h_r, h_i, w2r, b2r, w2i, b2i, We, be, g_r
             norm_first_half(last - 2, k)
             stage_2(last - 1, k)
         reciprocal_rms(last - 2, 0, TILES)
-        gain_scale_store(last - 3, 0, TILES)
+        gain_scale_store(last - 3, last, 0, TILES)
         for piece in range(PIECES):
             bias_and_round(last, piece)
         for k in range(TILES):
             norm_first_half(last - 1, k)
-        gain_scale_store(last - 2, 0, 1)
+        gain_scale_store(last - 2, last - 1, 0, 1)
         reciprocal_rms(last - 1, 0, TILES)
         quantise_cat(last, 0, TILES)
         for k in range(TILES):

@@ -22,6 +22,7 @@ TILES = 2
 STEP_TOKENS = TILES * P
 STEPS = TOKENS // STEP_TOKENS
 PIECES = TILES * STREAMS
+SCALAR_PIECE = 0
 EPS = 1e-6
 
 FLOPS = 2 * TOKENS * F * D * STREAMS + 2 * TOKENS * (STREAMS * D) * D
@@ -148,6 +149,7 @@ def tile_wavenetworklm_pb_t_kernel(tc, h_r, h_i, w2r, b2r, w2i, b2i, We, be, g_r
         sums_1 = {}
         cat_grouped = {}
         cat_codes = {}
+        by_feature = {}
         sums_2 = {}
         wave = {}
         square_sums = {}
@@ -219,6 +221,24 @@ def tile_wavenetworklm_pb_t_kernel(tc, h_r, h_i, w2r, b2r, w2i, b2i, We, be, g_r
                 in0=sums_1[(n, piece)][:].rearrange("p t r -> p r t"),
                 in1=b2[s][:].unsqueeze(1).to_broadcast([P, P, PACK]),
                 op=ADD,
+            )
+
+        def bias_and_round_on_scalar(n):
+            rounded = work.tile([P, PACK, P], BF16)
+            for t in range(PACK):
+                nc.scalar.activation(
+                    out=rounded[:, t, :],
+                    in_=sums_1[(n, SCALAR_PIECE)][:, t, :],
+                    func=ACT.Identity,
+                    bias=b2[SCALAR_PIECE % STREAMS][:, t : t + 1],
+                )
+            by_feature[n] = rounded
+
+        def interleave(n):
+            width = P * PACK
+            nc.vector.tensor_copy(
+                out=cat_grouped[n][:, SCALAR_PIECE * width : (SCALAR_PIECE + 1) * width].rearrange("p (r t) -> p r t", t=PACK),
+                in_=by_feature[n][:].rearrange("p t r -> p r t"),
             )
 
         def quantise_cat(n, first, last):
@@ -361,6 +381,7 @@ def tile_wavenetworklm_pb_t_kernel(tc, h_r, h_i, w2r, b2r, w2i, b2i, We, be, g_r
             new_cat(i)
             for s in range(STREAMS):
                 copy_h(i + 1, s)
+            bias_and_round_on_scalar(i)
             new_norm(i - 2)
             for k in range(TILES):
                 norm_first_half(i - 2, k)
@@ -372,7 +393,9 @@ def tile_wavenetworklm_pb_t_kernel(tc, h_r, h_i, w2r, b2r, w2i, b2i, We, be, g_r
                 for s in range(STREAMS):
                     transposes(i + 2, s)
             for piece in range(PIECES):
-                bias_and_round(i, piece)
+                if piece != SCALAR_PIECE:
+                    bias_and_round(i, piece)
+            interleave(i)
             quantise_h(i + 1, 0, STREAMS)
             for piece in range(PIECES):
                 stage_1(i + 1, piece)

@@ -23,6 +23,7 @@ STEP_TOKENS = TILES * P
 STEPS = TOKENS // STEP_TOKENS
 PIECES = TILES * STREAMS
 SCALAR_PIECE = 0
+NEIGHBOURS = 4
 EPS = 1e-6
 
 FLOPS = 2 * TOKENS * F * D * STREAMS + 2 * TOKENS * (STREAMS * D) * D
@@ -134,8 +135,10 @@ def tile_wavenetworklm_pb_t_kernel(tc, h_r, h_i, w2r, b2r, w2i, b2i, We, be, g_r
         def regroup_we(copy, s, first, last):
             columns = slice(first * (D // 8), last * (D // 8))
             copy(
-                out=we_grouped[:, s, :].rearrange("p (d t) -> p d t", t=PACK)[:, columns],
-                in_=we_raw[s][:].rearrange("p t d -> p d t")[:, columns],
+                out=we_grouped[:, s, columns.start * PACK : columns.stop * PACK].rearrange(
+                    "p (c i t) -> p c t i", i=NEIGHBOURS, t=PACK
+                ),
+                in_=we_raw[s][:, :, columns].rearrange("p t (c i) -> p c t i", i=NEIGHBOURS),
             )
 
         def quantise_we(s):
@@ -237,8 +240,10 @@ def tile_wavenetworklm_pb_t_kernel(tc, h_r, h_i, w2r, b2r, w2i, b2i, We, be, g_r
         def interleave(n):
             width = P * PACK
             nc.vector.tensor_copy(
-                out=cat_grouped[n][:, SCALAR_PIECE * width : (SCALAR_PIECE + 1) * width].rearrange("p (r t) -> p r t", t=PACK),
-                in_=by_feature[n][:].rearrange("p t r -> p r t"),
+                out=cat_grouped[n][:, SCALAR_PIECE * width : (SCALAR_PIECE + 1) * width].rearrange(
+                    "p (c i t) -> p c t i", i=NEIGHBOURS, t=PACK
+                ),
+                in_=by_feature[n][:].rearrange("p t (c i) -> p c t i", i=NEIGHBOURS),
             )
 
         def quantise_cat(n, first, last):
@@ -338,7 +343,7 @@ def tile_wavenetworklm_pb_t_kernel(tc, h_r, h_i, w2r, b2r, w2i, b2i, We, be, g_r
             stage_1(0, k * STREAMS)
         quantise_w2(1)
         quantise_h(0, 1, STREAMS)
-        regroup_we(nc.scalar.copy, 0, 0, 4)
+        regroup_we(nc.scalar.copy, 0, 0, 8)
         for k in range(TILES):
             bias_and_round(0, k * STREAMS)
         for k in range(TILES):
@@ -348,9 +353,8 @@ def tile_wavenetworklm_pb_t_kernel(tc, h_r, h_i, w2r, b2r, w2i, b2i, We, be, g_r
             copy_h(1, s)
         for k in range(TILES):
             bias_and_round(0, k * STREAMS + 1)
-        regroup_we(nc.vector.tensor_copy, 1, 0, 6)
-        regroup_we(nc.scalar.copy, 0, 4, 8)
-        regroup_we(nc.scalar.copy, 1, 6, 8)
+        regroup_we(nc.vector.tensor_copy, 1, 0, 4)
+        regroup_we(nc.scalar.copy, 1, 4, 8)
         quantise_h(1, 0, STREAMS)
         new_h(2)
         transposes(2, 0)
@@ -386,9 +390,9 @@ def tile_wavenetworklm_pb_t_kernel(tc, h_r, h_i, w2r, b2r, w2i, b2i, We, be, g_r
             for k in range(TILES):
                 norm_first_half(i - 2, k)
                 stage_2(i - 1, k)
-            reciprocal_rms(i - 2, 0, TILES)
             if i > 2:
                 gain_scale_store(i - 3, i, 0, TILES)
+            reciprocal_rms(i - 2, 0, TILES)
             if i + 2 < STEPS:
                 for s in range(STREAMS):
                     transposes(i + 2, s)
@@ -408,8 +412,8 @@ def tile_wavenetworklm_pb_t_kernel(tc, h_r, h_i, w2r, b2r, w2i, b2i, We, be, g_r
         for k in range(TILES):
             norm_first_half(last - 2, k)
             stage_2(last - 1, k)
-        reciprocal_rms(last - 2, 0, TILES)
         gain_scale_store(last - 3, last, 0, TILES)
+        reciprocal_rms(last - 2, 0, TILES)
         for piece in range(PIECES):
             bias_and_round(last, piece)
         for k in range(TILES):

from contextlib import ExitStack

import concourse.mybir as mybir
from concourse.masks import make_identity

F32 = mybir.dt.float32
BF16 = mybir.dt.bfloat16
U32 = mybir.dt.uint32
U8 = mybir.dt.uint8
FP8X4 = mybir.dt.float8_e4m3fn_x4
ADD = mybir.AluOpType.add
MULT = mybir.AluOpType.mult
ACT = mybir.ActivationFunctionType

P = 128
PACK = 4
TOKENS = 4096
F = 512
D = 512
STREAMS = 2
TILES = 2
STEP_TOKENS = TILES * P
STEPS = TOKENS // STEP_TOKENS
PIECES = TILES * STREAMS
SCALAR_PIECE = 0
NEIGHBOURS = 4
EPS = 1e-6

FLOPS = 2 * TOKENS * F * D * STREAMS + 2 * TOKENS * (STREAMS * D) * D


def tile_wavenetworklm_pb_t_kernel(tc, h_r, h_i, w2r, b2r, w2i, b2i, We, be, g_rms, out):
    nc = tc.nc
    h_dram = [h_r.flatten_outer_dims(), h_i.flatten_outer_dims()]
    w2_dram = [w2r, w2i]
    b2_dram = [b2r, b2i]
    out_dram = out.flatten_outer_dims()

    with ExitStack() as stack:
        stack.enter_context(tc.manual_schedule())
        keep = stack.enter_context(tc.tile_pool(name="keep", bufs=1))
        work = stack.enter_context(tc.tile_pool(name="work", bufs=2))
        tail = stack.enter_context(tc.tile_pool(name="tail", bufs=4))
        psum_t = stack.enter_context(tc.psum_pool(name="psum_t", bufs=2))
        psum_1 = stack.enter_context(tc.psum_pool(name="psum_1", bufs=4))
        psum_2 = stack.enter_context(tc.psum_pool(name="psum_2", bufs=2))

        def load_h(n, s):
            rows = slice(n * STEP_TOKENS, (n + 1) * STEP_TOKENS)
            h_sb = keep.tile([P, TILES * F], BF16, name="h_%d_%d" % (s, n))
            nc.sync.dma_start(out=h_sb[:], in_=h_dram[s][rows, :].rearrange("(p k) f -> p (k f)", k=TILES))
            h_tiles[(n, s)] = h_sb

        def load_w2(s):
            raw = keep.tile([P, PACK, D], BF16, name="w2_raw_%d" % s)
            nc.sync.dma_start(
                out=raw[:].rearrange("q j d -> q (j d)"),
                in_=w2_dram[s].rearrange("(q j) d -> q (j d)", j=PACK),
            )
            return raw

        be_all = keep.tile([P, D], BF16)
        gain_all = keep.tile([P, TILES, D], BF16)
        w2_raw = []
        h_tiles = {}
        for s in range(STREAMS):
            w2_raw.append(load_w2(s))
            load_h(0, s)
        we_raw = []
        for s in range(STREAMS):
            half = keep.tile([P, PACK, D], BF16, name="we_raw_%d" % s)
            nc.sync.dma_start(
                out=half[:].rearrange("p t d -> p (t d)"),
                in_=We[s * D : (s + 1) * D, :].rearrange("(p t) d -> p (t d)", t=PACK),
            )
            we_raw.append(half)
            for stream in range(STREAMS):
                load_h(1 + s, stream)
        for n in range(3, STEPS):
            for s in range(STREAMS):
                load_h(n, s)

        identity = keep.tile([P, P], F32)
        make_identity(nc, identity[:])
        eps = keep.tile([P, 1], F32)
        nc.vector.memset(eps[:], EPS)
        unused = keep.tile([P, 1], F32)
        nc.scalar.activation(out=unused[:], in_=eps[:], func=ACT.Abs_reciprocal_sqrt)

        rows = keep.tile([P, 2, D], BF16)
        ones = keep.tile([P, P], BF16)
        nc.vector.memset(rows[:].rearrange("p v d -> p (v d)").bitcast(U32), 0)
        nc.vector.memset(ones[:], 1.0)

        b2 = []
        for s in range(STREAMS):
            b2_sb = keep.tile([P, PACK], BF16, name="b2_%d" % s)
            nc.scalar.dma_start(out=b2_sb[:], in_=b2_dram[s].rearrange("(p t) -> p t", t=PACK))
            b2.append(b2_sb)
        for v, vector in enumerate((be, g_rms)):
            nc.scalar.dma_start(out=rows[0:1, v, :], in_=vector.unsqueeze(0))

        def spread_rows():
            for v, copies in enumerate(((be_all[:],), [gain_all[:, k, :] for k in range(TILES)])):
                sums = psum_2.tile([P, D], F32)
                nc.tensor.matmul(out=sums[:], lhsT=ones[:], rhs=rows[:, v, :], start=True, stop=True)
                for spread in copies:
                    nc.scalar.copy(out=spread, in_=sums[:])

        w2_codes = []
        w2_scales = []

        w2_grouped = []
        for s in range(STREAMS):
            grouped = keep.tile([P, D * PACK], BF16, name="w2_grouped_%d" % s, align_bytes=64)
            codes = keep.tile([P, D], U32, name="w2_codes_%d" % s, align_bytes=64)
            scales = keep.tile([P, D], U8, name="w2_scales_%d" % s, align_bytes=64)
            w2_grouped.append(grouped)
            w2_codes.append(codes)
            w2_scales.append(scales)

        def regroup_w2(copy, s, first, last):
            copy(
                out=w2_grouped[s][:].rearrange("q (t c j) -> q t c j", t=PACK, j=PACK)[:, first:last],
                in_=w2_raw[s][:].rearrange("q j (c t) -> q t c j", t=PACK)[:, first:last],
            )

        def quantise_w2(s):
            nc.vector.quantize_mx(out=w2_codes[s][:].bitcast(FP8X4), scales=w2_scales[s][:], in_=w2_grouped[s][:])

        we_grouped = keep.tile([P, STREAMS, D * PACK], BF16, align_bytes=64)
        we_codes = keep.tile([P, STREAMS, D], U32, align_bytes=64)
        we_scales = keep.tile([P, STREAMS, D], U8, align_bytes=64)

        def regroup_we(copy, s, first, last):
            columns = slice(first * (D // 8), last * (D // 8))
            copy(
                out=we_grouped[:, s, columns.start * PACK : columns.stop * PACK].rearrange(
                    "p (c i t) -> p c t i", i=NEIGHBOURS, t=PACK
                ),
                in_=we_raw[s][:, :, columns].rearrange("p t (c i) -> p c t i", i=NEIGHBOURS),
            )

        def quantise_we(s):
            nc.vector.quantize_mx(
                out=we_codes[:, s, :].bitcast(FP8X4), scales=we_scales[:, s, :], in_=we_grouped[:, s, :]
            )

        h_words = {}
        h_grouped = {}
        h_codes = {}
        sums_1 = {}
        cat_grouped = {}
        cat_codes = {}
        by_feature = {}
        sums_2 = {}
        wave = {}
        square_sums = {}
        inv_rms = {}

        def transposes(n, s):
            words = psum_t.tile([P, TILES, 2, P], F32)
            source = h_tiles[(n, s)][:].bitcast(F32)
            for k in range(TILES):
                for u in range(2):
                    token = slice(k * (F // 2) + u, (k + 1) * (F // 2), 2)
                    nc.tensor.transpose(words[:, k, u, :], source[:, token], identity[:])
            h_words[(n, s)] = words

        def new_h(n):
            grouped = work.tile([P, PIECES * P * PACK], BF16, name="h_grouped", bufs=3, align_bytes=64)
            codes = work.tile([P, PIECES * P], U32, name="h_codes", align_bytes=64)
            scales = work.tile([P, PIECES * P], U8, name="h_scales", align_bytes=64)
            h_grouped[n] = grouped
            h_codes[n] = (codes, scales)

        def copy_h(n, s):
            width = TILES * P * 2
            nc.scalar.copy(
                out=h_grouped[n][:].bitcast(F32)[:, s * width : (s + 1) * width].rearrange("p (k r u) -> p k r u", k=TILES, u=2),
                in_=h_words[(n, s)][:].rearrange("p k u r -> p k r u"),
            )

        def quantise_h(n, first, last):
            codes, scales = h_codes[n]
            words = slice(first * TILES * P, last * TILES * P)
            nc.vector.quantize_mx(
                out=codes[:, words].bitcast(FP8X4),
                scales=scales[:, words],
                in_=h_grouped[n][:, first * TILES * P * PACK : last * TILES * P * PACK],
            )

        def stage_1(n, piece):
            k, s = divmod(piece, STREAMS)
            codes, scales = h_codes[n]
            first = (s * TILES + k) * P
            tokens = slice(first, first + P)
            sums = psum_1.tile([P, PACK, P], F32)
            for t in range(PACK):
                columns = slice(t * P, (t + 1) * P)
                nc.tensor.matmul_mx(
                    out=sums[:, t, :],
                    lhsT=w2_codes[s][:, columns].bitcast(FP8X4),
                    lhsT_scale=w2_scales[s][:, columns],
                    rhs=codes[:, tokens].bitcast(FP8X4),
                    rhs_scale=scales[:, tokens],
                    start=True,
                    stop=True,
                )
            sums_1[(n, piece)] = sums

        def new_cat(n):
            cat = work.tile([P, PIECES * P * PACK], BF16, align_bytes=64)
            codes = work.tile([P, PIECES * P], U32, name="cat_codes", align_bytes=64)
            scales = work.tile([P, PIECES * P], U8, name="cat_scales", align_bytes=64)
            cat_grouped[n] = cat
            cat_codes[n] = (codes, scales)

        def bias_and_round(n, piece):
            s = piece % STREAMS
            width = P * PACK
            nc.vector.tensor_tensor(
                out=cat_grouped[n][:, piece * width : (piece + 1) * width].rearrange("p (r t) -> p r t", t=PACK),
                in0=sums_1[(n, piece)][:].rearrange("p t r -> p r t"),
                in1=b2[s][:].unsqueeze(1).to_broadcast([P, P, PACK]),
                op=ADD,
            )

        def bias_and_round_on_scalar(n):
            rounded = work.tile([P, PACK, P], BF16)
            for t in range(PACK):
                nc.scalar.activation(
                    out=rounded[:, t, :],
                    in_=sums_1[(n, SCALAR_PIECE)][:, t, :],
                    func=ACT.Identity,
                    bias=b2[SCALAR_PIECE % STREAMS][:, t : t + 1],
                )
            by_feature[n] = rounded

        def interleave(n):
            width = P * PACK
            nc.vector.tensor_copy(
                out=cat_grouped[n][:, SCALAR_PIECE * width : (SCALAR_PIECE + 1) * width].rearrange(
                    "p (c i t) -> p c t i", i=NEIGHBOURS, t=PACK
                ),
                in_=by_feature[n][:].rearrange("p t (c i) -> p c t i", i=NEIGHBOURS),
            )

        def quantise_cat(n, first, last):
            codes, scales = cat_codes[n]
            words = slice(first * STREAMS * P, last * STREAMS * P)
            nc.vector.quantize_mx(
                out=codes[:, words].bitcast(FP8X4),
                scales=scales[:, words],
                in_=cat_grouped[n][:, first * STREAMS * P * PACK : last * STREAMS * P * PACK],
            )

        def stage_2(n, k):
            codes, scales = cat_codes[n]
            sums = psum_2.tile([P, D], F32)
            for s in range(STREAMS):
                tokens = slice((k * STREAMS + s) * P, (k * STREAMS + s + 1) * P)
                nc.tensor.matmul_mx(
                    out=sums[:],
                    lhsT=codes[:, tokens].bitcast(FP8X4),
                    lhsT_scale=scales[:, tokens],
                    rhs=we_codes[:, s, :].bitcast(FP8X4),
                    rhs_scale=we_scales[:, s, :],
                    start=(s == 0),
                    stop=(s == STREAMS - 1),
                )
            sums_2[(n, k)] = sums

        def new_norm(n):
            biased = tail.tile([P, TILES, D], F32)
            totals = tail.tile([P, TILES], F32)
            factors = tail.tile([P, TILES], F32)
            wave[n] = biased
            square_sums[n] = totals
            inv_rms[n] = factors

        def norm_first_half(n, k):
            nc.vector.tensor_tensor(out=wave[n][:, k, :], in0=sums_2[(n, k)][:], in1=be_all[:], op=ADD)
            squares = work.tile([P, D], BF16)
            nc.scalar.activation(
                out=squares[:], in_=wave[n][:, k, :], func=ACT.Square, accum_out=square_sums[n][:, k : k + 1]
            )

        def reciprocal_rms(n, first, last):
            nc.scalar.activation(
                out=inv_rms[n][:, first:last],
                in_=square_sums[n][:, first:last],
                func=ACT.Abs_reciprocal_sqrt,
                scale=1.0 / D,
                bias=eps[:],
            )

        def out_rows(n):
            return out_dram[n * STEP_TOKENS : (n + 1) * STEP_TOKENS, :].rearrange("(p k) d -> p k d", k=TILES)

        def gain_scale_store(n, spent, first, last):
            with_gain = h_grouped[spent][:].bitcast(F32).rearrange("p (k d) -> p k d", k=TILES)
            result = tail.tile([P, TILES, D], F32)
            nc.gpsimd.tensor_tensor(
                out=with_gain[:, first:last, :],
                in0=wave[n][:, first:last, :],
                in1=gain_all[:, first:last, :],
                op=MULT,
            )
            for k in range(first, last):
                nc.scalar.activation(
                    out=result[:, k, :], in_=with_gain[:, k, :], func=ACT.Copy, scale=inv_rms[n][:, k : k + 1]
                )
                nc.sync.dma_start(out=out_rows(n)[:, k, :], in_=result[:, k, :])

        def gain_scale_store_on_vector(n, k):
            result = tail.tile([P, D], F32, name="last_result", bufs=3 * TILES)
            nc.vector.scalar_tensor_tensor(
                out=result[:],
                in0=wave[n][:, k, :],
                scalar=inv_rms[n][:, k : k + 1],
                in1=gain_all[:, k, :],
                op0=MULT,
                op1=MULT,
            )
            nc.sync.dma_start(out=out_rows(n)[:, k, :], in_=result[:])

        new_h(0)
        new_h(1)
        new_cat(0)
        transposes(0, 0)
        regroup_w2(nc.scalar.copy, 0, 2, PACK)
        regroup_w2(nc.vector.tensor_copy, 0, 0, 2)
        copy_h(0, 0)
        quantise_w2(0)
        regroup_w2(nc.scalar.copy, 1, 3, PACK)
        regroup_w2(nc.vector.tensor_copy, 1, 0, 1)
        quantise_h(0, 0, 1)
        regroup_w2(nc.vector.tensor_copy, 1, 1, 3)
        transposes(0, 1)
        copy_h(0, 1)
        for k in range(TILES):
            stage_1(0, k * STREAMS)
        quantise_w2(1)
        quantise_h(0, 1, STREAMS)
        regroup_we(nc.scalar.copy, 0, 0, 8)
        for k in range(TILES):
            bias_and_round(0, k * STREAMS)
        for k in range(TILES):
            stage_1(0, k * STREAMS + 1)
        for s in range(STREAMS):
            transposes(1, s)
            copy_h(1, s)
        for k in range(TILES):
            bias_and_round(0, k * STREAMS + 1)
        regroup_we(nc.vector.tensor_copy, 1, 0, 4)
        regroup_we(nc.scalar.copy, 1, 4, 8)
        quantise_h(1, 0, STREAMS)
        new_h(2)
        transposes(2, 0)
        transposes(2, 1)
        for piece in range(PIECES):
            stage_1(1, piece)
        quantise_cat(0, 0, TILES)
        for s in range(STREAMS):
            copy_h(2, s)

        new_cat(1)
        for piece in range(PIECES):
            bias_and_round(1, piece)
        spread_rows()
        quantise_h(2, 0, STREAMS)
        for s in range(STREAMS):
            quantise_we(s)
        quantise_cat(1, 0, TILES)
        for s in range(STREAMS):
            transposes(3, s)
        for k in range(TILES):
            stage_2(0, k)
        for piece in range(PIECES):
            stage_1(2, piece)

        for i in range(2, STEPS - 1):
            new_h(i + 1)
            new_cat(i)
            for s in range(STREAMS):
                copy_h(i + 1, s)
            bias_and_round_on_scalar(i)
            new_norm(i - 2)
            for k in range(TILES):
                norm_first_half(i - 2, k)
                stage_2(i - 1, k)
            if i > 2:
                gain_scale_store(i - 3, i, 0, TILES)
            reciprocal_rms(i - 2, 0, TILES)
            if i + 2 < STEPS:
                for s in range(STREAMS):
                    transposes(i + 2, s)
            for piece in range(PIECES):
                if piece != SCALAR_PIECE:
                    bias_and_round(i, piece)
            interleave(i)
            quantise_h(i + 1, 0, STREAMS)
            for piece in range(PIECES):
                stage_1(i + 1, piece)
            quantise_cat(i, 0, TILES)

        last = STEPS - 1
        new_cat(last)
        for n in range(last - 2, last + 1):
            new_norm(n)
        for k in range(TILES):
            norm_first_half(last - 2, k)
            stage_2(last - 1, k)
        gain_scale_store(last - 3, last, 0, TILES)
        reciprocal_rms(last - 2, 0, TILES)
        for piece in range(PIECES):
            bias_and_round(last, piece)
        for k in range(TILES):
            norm_first_half(last - 1, k)
        gain_scale_store(last - 2, last - 1, 0, 1)
        reciprocal_rms(last - 1, 0, TILES)
        quantise_cat(last, 0, TILES)
        for k in range(TILES):
            stage_2(last, k)
        gain_scale_store_on_vector(last - 2, 1)
        for k in range(TILES):
            norm_first_half(last, k)
            reciprocal_rms(last, k, k + 1)
        for n in range(last - 1, last + 1):
            for k in range(TILES):
                gain_scale_store_on_vector(n, k)
